import numpy as np
import ml_dtypes

BF16 = ml_dtypes.bfloat16


def bf(x):
    return np.asarray(x, np.float32).astype(BF16)


def f32(x):
    return np.asarray(x, np.float32)


def f64(x):
    return np.asarray(x).astype(np.float64)


def striped(idx):
    return np.tile(idx.reshape(-1, 16).T, (8, 1))


S, D, M, K, H, N = 256, 128, 256, 4, 128, 1024


def setup_inputs():
    idx = np.concatenate([np.random.permutation(S)[:H] for _ in range(N // H)])
    return {"table": bf(np.random.standard_normal((S, D))), "wr": bf(np.random.standard_normal((D, M)) / np.sqrt(D)), "wnr": bf(np.random.standard_normal((D, M)) / np.sqrt(D)), "offs": striped(idx)}


def reference(table, wr, wnr, offs):
    idx = offs[:16].T.reshape(-1)
    z = f64(table)
    own = f64(wr).T @ z.T
    nbr = (f64(wnr).T @ z[idx].T).reshape(M, K, S).sum(axis=1)
    return np.maximum(own + nbr / K, 0.0)

@@ -1,0 +1,66 @@
+import concourse.mybir as mybir
+from concourse.masks import make_identity
+
+BF16, F32, U16 = mybir.dt.bfloat16, mybir.dt.float32, mybir.dt.uint16
+MULT, MAX = mybir.AluOpType.mult, mybir.AluOpType.max
+
+P = 128
+S = 256
+M = 256
+K = 4
+N = K * S
+PER_COLUMN = 16
+
+FLOPS = 2 * P * M * (S + N)
+
+
+def tile_residuesnetwork_kernel(tc, table, wr, wnr, offs, out):
+    nc = tc.nc
+    with (
+        tc.tile_pool(name="held", bufs=1) as held,
+        tc.psum_pool(name="psum", bufs=1) as psum,
+    ):
+        rows = held.tile([P, S // P, P], BF16, name="rows")
+        nc.sync.dma_start(rows[:], table.rearrange("(b p) d -> p b d", p=P))
+        offsets = held.tile([P, N // PER_COLUMN], U16, name="offsets")
+        nc.sync.dma_start(offsets[:], offs)
+        wnr_sb = held.tile([P, M], BF16, name="wnr_sb")
+        nc.scalar.dma_start(wnr_sb[:], wnr)
+        wr_sb = held.tile([P, M], BF16, name="wr_sb")
+        nc.scalar.dma_start(wr_sb[:], wr)
+
+        identity = held.tile([P, P], BF16, name="identity")
+        make_identity(nc, identity[:])
+        flipped = psum.tile([P, S], BF16, name="flipped")
+        for b in range(S // P):
+            nc.tensor.transpose(flipped[:, b * P : (b + 1) * P], rows[:, b, :], identity[:])
+        window = held.tile([P, S], BF16, name="window")
+        nc.vector.tensor_copy(window[:], flipped[:])
+
+        wr4 = held.tile([P, M], BF16, name="wr4")
+        nc.vector.tensor_scalar_mul(wr4[:], wr_sb[:], float(K))
+
+        blocks = [slice(mb * P, (mb + 1) * P) for mb in range(M // P)]
+        totals = [psum.tile([P, S], F32, name=f"total{mb}") for mb in range(M // P)]
+        for features, total in zip(blocks, totals):
+            nc.tensor.matmul(total[:], wr4[:, features], window[:], start=True, stop=False)
+
+        for mb, (features, total) in enumerate(zip(blocks, totals)):
+
+            def neighbours(first, count, start, stop):
+                picked = window[:].indirect(
+                    offsets[:, first // PER_COLUMN : (first + count) // PER_COLUMN]
+                )
+                nc.tensor.matmul(
+                    total[:, first % S : first % S + count], wnr_sb[:, features], picked,
+                    start=start, stop=stop,
+                )
+
+            for t in range(K - 1):
+                for half in range(2):
+                    neighbours(t * S + half * P, P, False, False)
+            neighbours((K - 1) * S, S, False, True)
+
+            result = held.tile([P, S], F32, name=f"result{mb}")
+            nc.vector.tensor_scalar(result[:], total[:], 1.0 / K, 0.0, MULT, MAX)
+            nc.sync.dma_start(out[features, :], result[:])

@@ -10,6 +10,8 @@ M = 256
 K = 4
 N = K * S
 PER_COLUMN = 16
+BANK = 512
+WARMING = 4
 
 FLOPS = 2 * P * M * (S + N)
 
@@ -28,6 +30,12 @@ def tile_residuesnetwork_kernel(tc, table, wr, wnr, offs, out):
         nc.scalar.dma_start(wnr_sb[:], wnr)
         wr_sb = held.tile([P, M], BF16, name="wr_sb")
         nc.scalar.dma_start(wr_sb[:], wr)
+
+        zeros = held.tile([P, BANK], BF16, name="zeros")
+        nc.vector.memset(zeros[:], 0.0)
+        unused = psum.tile([P, BANK], F32, name="unused")
+        for w in range(WARMING):
+            nc.tensor.matmul(unused[:], zeros[:, :P], zeros[:], start=True, stop=True)
 
         identity = held.tile([P, P], BF16, name="identity")
         make_identity(nc, identity[:])

@@ -2,7 +2,7 @@ import concourse.mybir as mybir
 from concourse.masks import make_identity
 
 BF16, F32, U16 = mybir.dt.bfloat16, mybir.dt.float32, mybir.dt.uint16
-MULT, MAX = mybir.AluOpType.mult, mybir.AluOpType.max
+MULT, ADD = mybir.AluOpType.mult, mybir.AluOpType.add
 
 P = 128
 S = 256
@@ -10,8 +10,6 @@ M = 256
 K = 4
 N = K * S
 PER_COLUMN = 16
-BANK = 512
-WARMING = 4
 
 FLOPS = 2 * P * M * (S + N)
 
@@ -31,12 +29,6 @@ def tile_residuesnetwork_kernel(tc, table, wr, wnr, offs, out):
         wr_sb = held.tile([P, M], BF16, name="wr_sb")
         nc.scalar.dma_start(wr_sb[:], wr)
 
-        zeros = held.tile([P, BANK], BF16, name="zeros")
-        nc.vector.memset(zeros[:], 0.0)
-        unused = psum.tile([P, BANK], F32, name="unused")
-        for w in range(WARMING):
-            nc.tensor.matmul(unused[:], zeros[:, :P], zeros[:], start=True, stop=True)
-
         identity = held.tile([P, P], BF16, name="identity")
         make_identity(nc, identity[:])
         flipped = psum.tile([P, S], BF16, name="flipped")
@@ -45,30 +37,30 @@ def tile_residuesnetwork_kernel(tc, table, wr, wnr, offs, out):
         window = held.tile([P, S], BF16, name="window")
         nc.vector.tensor_copy(window[:], flipped[:])
 
-        wr4 = held.tile([P, M], BF16, name="wr4")
-        nc.vector.tensor_scalar_mul(wr4[:], wr_sb[:], float(K))
-
         blocks = [slice(mb * P, (mb + 1) * P) for mb in range(M // P)]
-        totals = [psum.tile([P, S], F32, name=f"total{mb}") for mb in range(M // P)]
-        for features, total in zip(blocks, totals):
-            nc.tensor.matmul(total[:], wr4[:, features], window[:], start=True, stop=False)
+        owns = []
+        for mb, features in enumerate(blocks):
+            own_psum = psum.tile([P, S], F32, name=f"own_psum{mb}")
+            nc.tensor.matmul(own_psum[:], wr_sb[:, features], window[:], start=True, stop=True)
+            own = held.tile([P, S], F32, name=f"own{mb}")
+            nc.scalar.copy(own[:], own_psum[:])
+            owns.append(own)
 
-        for mb, (features, total) in enumerate(zip(blocks, totals)):
-
-            def neighbours(first, count, start, stop):
-                picked = window[:].indirect(
-                    offsets[:, first // PER_COLUMN : (first + count) // PER_COLUMN]
-                )
-                nc.tensor.matmul(
-                    total[:, first % S : first % S + count], wnr_sb[:, features], picked,
-                    start=start, stop=stop,
-                )
-
-            for t in range(K - 1):
-                for half in range(2):
-                    neighbours(t * S + half * P, P, False, False)
-            neighbours((K - 1) * S, S, False, True)
-
+        for mb, features in enumerate(blocks):
+            so_far = owns[mb]
+            for pair in range(K // 2):
+                both = psum.tile([P, S], F32, name=f"both{mb}{pair}")
+                for second in range(2):
+                    t = 2 * pair + second
+                    picked = window[:].indirect(
+                        offsets[:, t * S // PER_COLUMN : (t + 1) * S // PER_COLUMN]
+                    )
+                    nc.tensor.matmul(
+                        both[:], wnr_sb[:, features], picked, start=second == 0, stop=second == 1
+                    )
+                summed = held.tile([P, S], F32, name=f"summed{mb}{pair}")
+                nc.vector.scalar_tensor_tensor(summed[:], both[:], 1.0 / K, so_far[:], MULT, ADD)
+                so_far = summed
             result = held.tile([P, S], F32, name=f"result{mb}")
-            nc.vector.tensor_scalar(result[:], total[:], 1.0 / K, 0.0, MULT, MAX)
+            nc.vector.tensor_scalar_max(result[:], so_far[:], 0.0)
             nc.sync.dma_start(out[features, :], result[:])

@@ -2,7 +2,7 @@ import concourse.mybir as mybir
 from concourse.masks import make_identity
 
 BF16, F32, U16 = mybir.dt.bfloat16, mybir.dt.float32, mybir.dt.uint16
-MULT, ADD = mybir.AluOpType.mult, mybir.AluOpType.add
+MULT, MAX = mybir.AluOpType.mult, mybir.AluOpType.max
 
 P = 128
 S = 256
@@ -37,30 +37,25 @@ def tile_residuesnetwork_kernel(tc, table, wr, wnr, offs, out):
         window = held.tile([P, S], BF16, name="window")
         nc.vector.tensor_copy(window[:], flipped[:])
 
-        blocks = [slice(mb * P, (mb + 1) * P) for mb in range(M // P)]
-        owns = []
-        for mb, features in enumerate(blocks):
-            own_psum = psum.tile([P, S], F32, name=f"own_psum{mb}")
-            nc.tensor.matmul(own_psum[:], wr_sb[:, features], window[:], start=True, stop=True)
-            own = held.tile([P, S], F32, name=f"own{mb}")
-            nc.scalar.copy(own[:], own_psum[:])
-            owns.append(own)
+        wr4 = held.tile([P, M], BF16, name="wr4")
+        nc.vector.tensor_scalar_mul(wr4[:], wr_sb[:], float(K))
 
-        for mb, features in enumerate(blocks):
-            so_far = owns[mb]
-            for pair in range(K // 2):
-                both = psum.tile([P, S], F32, name=f"both{mb}{pair}")
-                for second in range(2):
-                    t = 2 * pair + second
-                    picked = window[:].indirect(
-                        offsets[:, t * S // PER_COLUMN : (t + 1) * S // PER_COLUMN]
-                    )
-                    nc.tensor.matmul(
-                        both[:], wnr_sb[:, features], picked, start=second == 0, stop=second == 1
-                    )
-                summed = held.tile([P, S], F32, name=f"summed{mb}{pair}")
-                nc.vector.scalar_tensor_tensor(summed[:], both[:], 1.0 / K, so_far[:], MULT, ADD)
-                so_far = summed
-            result = held.tile([P, S], F32, name=f"result{mb}")
-            nc.vector.tensor_scalar_max(result[:], so_far[:], 0.0)
-            nc.sync.dma_start(out[features, :], result[:])
+        quarters = [(mb * P, nb * P) for mb in range(M // P) for nb in range(S // P)]
+        totals = []
+        for q, (m0, n0) in enumerate(quarters):
+            total = psum.tile([P, P], F32, name=f"total{q}")
+            nc.tensor.matmul(
+                total[:], wr4[:, m0 : m0 + P], window[:, n0 : n0 + P], start=True, stop=False
+            )
+            totals.append(total)
+
+        for q, (m0, n0) in enumerate(quarters):
+            for t in range(K):
+                first = (t * S + n0) // PER_COLUMN
+                picked = window[:].indirect(offsets[:, first : first + P // PER_COLUMN])
+                nc.tensor.matmul(
+                    totals[q][:], wnr_sb[:, m0 : m0 + P], picked, start=False, stop=t == K - 1
+                )
+            result = held.tile([P, P], F32, name=f"result{q}")
+            nc.vector.tensor_scalar(result[:], totals[q][:], 1.0 / K, 0.0, MULT, MAX)
+            nc.sync.dma_start(out[m0 : m0 + P, n0 : n0 + P], result[:])

@@ -24,23 +24,23 @@ def tile_residuesnetwork_kernel(tc, table, wr, wnr, offs, out):
         nc.sync.dma_start(rows[:], table.rearrange("(b p) d -> p b d", p=P))
         offsets = held.tile([P, N // PER_COLUMN], U16, name="offsets")
         nc.sync.dma_start(offsets[:], offs)
-        wnr_sb = held.tile([P, M], BF16, name="wnr_sb")
-        nc.scalar.dma_start(wnr_sb[:], wnr)
         wr_sb = held.tile([P, M], BF16, name="wr_sb")
         nc.scalar.dma_start(wr_sb[:], wr)
-
-        identity = held.tile([P, P], BF16, name="identity")
-        make_identity(nc, identity[:])
-        flipped = psum.tile([P, S], BF16, name="flipped")
-        for b in range(S // P):
-            nc.tensor.transpose(flipped[:, b * P : (b + 1) * P], rows[:, b, :], identity[:])
-        window = held.tile([P, S], BF16, name="window")
-        nc.vector.tensor_copy(window[:], flipped[:])
+        wnr_sb = held.tile([P, M], BF16, name="wnr_sb")
+        nc.scalar.dma_start(wnr_sb[:], wnr)
 
         wr4 = held.tile([P, M], BF16, name="wr4")
         nc.vector.tensor_scalar_mul(wr4[:], wr_sb[:], float(K))
 
-        quarters = [(mb * P, nb * P) for mb in range(M // P) for nb in range(S // P)]
+        identity = held.tile([P, P], BF16, name="identity")
+        make_identity(nc, identity[:])
+        window = held.tile([P, S], BF16, name="window")
+        for b in range(S // P):
+            flipped = psum.tile([P, P], BF16, name=f"flipped{b}")
+            nc.tensor.transpose(flipped[:], rows[:, b, :], identity[:])
+            nc.vector.tensor_copy(window[:, b * P : (b + 1) * P], flipped[:])
+
+        quarters = [(mb * P, nb * P) for nb in range(S // P) for mb in range(M // P)]
         totals = []
         for q, (m0, n0) in enumerate(quarters):
             total = psum.tile([P, P], F32, name=f"total{q}")

@@ -20,8 +20,9 @@ def tile_residuesnetwork_kernel(tc, table, wr, wnr, offs, out):
         tc.tile_pool(name="held", bufs=1) as held,
         tc.psum_pool(name="psum", bufs=1) as psum,
     ):
-        rows = held.tile([P, S // P, P], BF16, name="rows")
-        nc.sync.dma_start(rows[:], table.rearrange("(b p) d -> p b d", p=P))
+        rows = [held.tile([P, P], BF16, name=f"rows{b}") for b in range(S // P)]
+        for b in range(S // P):
+            nc.sync.dma_start(rows[b][:], table[b * P : (b + 1) * P, :])
         offsets = held.tile([P, N // PER_COLUMN], U16, name="offsets")
         nc.sync.dma_start(offsets[:], offs)
         wr_sb = held.tile([P, M], BF16, name="wr_sb")
@@ -37,7 +38,7 @@ def tile_residuesnetwork_kernel(tc, table, wr, wnr, offs, out):
         window = held.tile([P, S], BF16, name="window")
         for b in range(S // P):
             flipped = psum.tile([P, P], BF16, name=f"flipped{b}")
-            nc.tensor.transpose(flipped[:], rows[:, b, :], identity[:])
+            nc.tensor.transpose(flipped[:], rows[b][:], identity[:])
             nc.vector.tensor_copy(window[:, b * P : (b + 1) * P], flipped[:])
 
         quarters = [(mb * P, nb * P) for nb in range(S // P) for mb in range(M // P)]
@@ -49,6 +50,7 @@ def tile_residuesnetwork_kernel(tc, table, wr, wnr, offs, out):
             )
             totals.append(total)
 
+        results = [held.tile([P, S], F32, name=f"result{mb}") for mb in range(M // P)]
         for q, (m0, n0) in enumerate(quarters):
             for t in range(K):
                 first = (t * S + n0) // PER_COLUMN
@@ -56,6 +58,9 @@ def tile_residuesnetwork_kernel(tc, table, wr, wnr, offs, out):
                 nc.tensor.matmul(
                     totals[q][:], wnr_sb[:, m0 : m0 + P], picked, start=False, stop=t == K - 1
                 )
-            result = held.tile([P, P], F32, name=f"result{q}")
-            nc.vector.tensor_scalar(result[:], totals[q][:], 1.0 / K, 0.0, MULT, MAX)
-            nc.sync.dma_start(out[m0 : m0 + P, n0 : n0 + P], result[:])
+            result = results[m0 // P]
+            nc.vector.tensor_scalar(result[:, n0 : n0 + P], totals[q][:], 1.0 / K, 0.0, MULT, MAX)
+            if m0 + P == M:
+                nc.sync.dma_start(out[m0 : m0 + P, n0 : n0 + P], result[:, n0 : n0 + P])
+            elif n0 + P == S:
+                nc.sync.dma_start(out[m0 : m0 + P, :], result[:])

@@ -41,26 +41,27 @@ def tile_residuesnetwork_kernel(tc, table, wr, wnr, offs, out):
             nc.tensor.transpose(flipped[:], rows[b][:], identity[:])
             nc.vector.tensor_copy(window[:, b * P : (b + 1) * P], flipped[:])
 
-        quarters = [(mb * P, nb * P) for nb in range(S // P) for mb in range(M // P)]
-        totals = []
-        for q, (m0, n0) in enumerate(quarters):
-            total = psum.tile([P, P], F32, name=f"total{q}")
-            nc.tensor.matmul(
-                total[:], wr4[:, m0 : m0 + P], window[:, n0 : n0 + P], start=True, stop=False
-            )
-            totals.append(total)
-
-        results = [held.tile([P, S], F32, name=f"result{mb}") for mb in range(M // P)]
-        for q, (m0, n0) in enumerate(quarters):
-            for t in range(K):
-                first = (t * S + n0) // PER_COLUMN
-                picked = window[:].indirect(offsets[:, first : first + P // PER_COLUMN])
+        totals = {}
+        for n0 in range(0, S, P):
+            for m0 in range(0, M, P):
+                total = psum.tile([P, P], F32, name=f"total_{m0}_{n0}")
                 nc.tensor.matmul(
-                    totals[q][:], wnr_sb[:, m0 : m0 + P], picked, start=False, stop=t == K - 1
+                    total[:], wr4[:, m0 : m0 + P], window[:, n0 : n0 + P], start=True, stop=False
                 )
-            result = results[m0 // P]
-            nc.vector.tensor_scalar(result[:, n0 : n0 + P], totals[q][:], 1.0 / K, 0.0, MULT, MAX)
-            if m0 + P == M:
-                nc.sync.dma_start(out[m0 : m0 + P, n0 : n0 + P], result[:, n0 : n0 + P])
-            elif n0 + P == S:
-                nc.sync.dma_start(out[m0 : m0 + P, :], result[:])
+                totals[m0, n0] = total
+
+        for m0 in range(0, M, P):
+            result = held.tile([P, S], F32, name=f"result_{m0}")
+            for n0 in range(0, S, P):
+                total = totals[m0, n0]
+                for t in range(K):
+                    first = (t * S + n0) // PER_COLUMN
+                    picked = window[:].indirect(offsets[:, first : first + P // PER_COLUMN])
+                    nc.tensor.matmul(
+                        total[:], wnr_sb[:, m0 : m0 + P], picked, start=False, stop=t == K - 1
+                    )
+                nc.vector.tensor_scalar(result[:, n0 : n0 + P], total[:], 1.0 / K, 0.0, MULT, MAX)
+                if m0 + P == M:
+                    nc.sync.dma_start(out[m0 : m0 + P, n0 : n0 + P], result[:, n0 : n0 + P])
+                elif n0 + P == S:
+                    nc.sync.dma_start(out[m0 : m0 + P, :], result[:])

@@ -41,27 +41,32 @@ def tile_residuesnetwork_kernel(tc, table, wr, wnr, offs, out):
             nc.tensor.transpose(flipped[:], rows[b][:], identity[:])
             nc.vector.tensor_copy(window[:, b * P : (b + 1) * P], flipped[:])
 
-        totals = {}
-        for n0 in range(0, S, P):
-            for m0 in range(0, M, P):
-                total = psum.tile([P, P], F32, name=f"total_{m0}_{n0}")
-                nc.tensor.matmul(
-                    total[:], wr4[:, m0 : m0 + P], window[:, n0 : n0 + P], start=True, stop=False
-                )
-                totals[m0, n0] = total
+        def picked(t, n0, width):
+            first = (t * S + n0) // PER_COLUMN
+            return window[:].indirect(offsets[:, first : first + width // PER_COLUMN])
 
-        for m0 in range(0, M, P):
-            result = held.tile([P, S], F32, name=f"result_{m0}")
+        block = psum.tile([P, S], F32, name="block")
+        halves = [psum.tile([P, P], F32, name=f"half{h}") for h in range(S // P)]
+
+        nc.tensor.matmul(halves[0][:], wr4[:, P:M], window[:, 0:P], start=True, stop=False)
+        nc.tensor.matmul(block[:], wr4[:, 0:P], window[:], start=True, stop=False)
+        nc.tensor.matmul(halves[1][:], wr4[:, P:M], window[:, P:S], start=True, stop=False)
+
+        for t in range(K - 1):
             for n0 in range(0, S, P):
-                total = totals[m0, n0]
-                for t in range(K):
-                    first = (t * S + n0) // PER_COLUMN
-                    picked = window[:].indirect(offsets[:, first : first + P // PER_COLUMN])
-                    nc.tensor.matmul(
-                        total[:], wnr_sb[:, m0 : m0 + P], picked, start=False, stop=t == K - 1
-                    )
-                nc.vector.tensor_scalar(result[:, n0 : n0 + P], total[:], 1.0 / K, 0.0, MULT, MAX)
-                if m0 + P == M:
-                    nc.sync.dma_start(out[m0 : m0 + P, n0 : n0 + P], result[:, n0 : n0 + P])
-                elif n0 + P == S:
-                    nc.sync.dma_start(out[m0 : m0 + P, :], result[:])
+                nc.tensor.matmul(
+                    block[:, n0 : n0 + P], wnr_sb[:, 0:P], picked(t, n0, P), start=False, stop=False
+                )
+        nc.tensor.matmul(block[:], wnr_sb[:, 0:P], picked(K - 1, 0, S), start=False, stop=True)
+        wide = held.tile([P, S], F32, name="wide")
+        nc.vector.tensor_scalar(wide[:], block[:], 1.0 / K, 0.0, MULT, MAX)
+        nc.sync.dma_start(out[0:P, :], wide[:])
+
+        for h, total in enumerate(halves):
+            for t in range(K):
+                nc.tensor.matmul(
+                    total[:], wnr_sb[:, P:M], picked(t, h * P, P), start=False, stop=t == K - 1
+                )
+            result = held.tile([P, P], F32, name=f"result{h}")
+            nc.vector.tensor_scalar(result[:], total[:], 1.0 / K, 0.0, MULT, MAX)
+            nc.sync.dma_start(out[P:M, h * P : (h + 1) * P], result[:])

@@ -48,9 +48,11 @@ def tile_residuesnetwork_kernel(tc, table, wr, wnr, offs, out):
         block = psum.tile([P, S], F32, name="block")
         halves = [psum.tile([P, P], F32, name=f"half{h}") for h in range(S // P)]
 
-        nc.tensor.matmul(halves[0][:], wr4[:, P:M], window[:, 0:P], start=True, stop=False)
-        nc.tensor.matmul(block[:], wr4[:, 0:P], window[:], start=True, stop=False)
-        nc.tensor.matmul(halves[1][:], wr4[:, P:M], window[:, P:S], start=True, stop=False)
+        for h, n0 in enumerate(range(0, S, P)):
+            nc.tensor.matmul(
+                block[:, n0 : n0 + P], wr4[:, 0:P], window[:, n0 : n0 + P], start=h == 0, stop=False
+            )
+            nc.tensor.matmul(halves[h][:], wr4[:, P:M], window[:, n0 : n0 + P], start=True, stop=False)
 
         for t in range(K - 1):
             for n0 in range(0, S, P):

@@ -2,7 +2,6 @@ import concourse.mybir as mybir
 from concourse.masks import make_identity
 
 BF16, F32, U16 = mybir.dt.bfloat16, mybir.dt.float32, mybir.dt.uint16
-MULT, MAX = mybir.AluOpType.mult, mybir.AluOpType.max
 
 P = 128
 S = 256
@@ -30,8 +29,8 @@ def tile_residuesnetwork_kernel(tc, table, wr, wnr, offs, out):
         wnr_sb = held.tile([P, M], BF16, name="wnr_sb")
         nc.scalar.dma_start(wnr_sb[:], wnr)
 
-        wr4 = held.tile([P, M], BF16, name="wr4")
-        nc.vector.tensor_scalar_mul(wr4[:], wr_sb[:], float(K))
+        wnr_quarter = held.tile([P, M], BF16, name="wnr_quarter")
+        nc.scalar.mul(wnr_quarter[:], wnr_sb[:], 1.0 / K)
 
         identity = held.tile([P, P], BF16, name="identity")
         make_identity(nc, identity[:])
@@ -50,25 +49,25 @@ def tile_residuesnetwork_kernel(tc, table, wr, wnr, offs, out):
 
         for h, n0 in enumerate(range(0, S, P)):
             nc.tensor.matmul(
-                block[:, n0 : n0 + P], wr4[:, 0:P], window[:, n0 : n0 + P], start=h == 0, stop=False
+                block[:, n0 : n0 + P], wr_sb[:, 0:P], window[:, n0 : n0 + P], start=h == 0, stop=False
             )
-            nc.tensor.matmul(halves[h][:], wr4[:, P:M], window[:, n0 : n0 + P], start=True, stop=False)
+            nc.tensor.matmul(halves[h][:], wr_sb[:, P:M], window[:, n0 : n0 + P], start=True, stop=False)
 
         for t in range(K - 1):
             for n0 in range(0, S, P):
                 nc.tensor.matmul(
-                    block[:, n0 : n0 + P], wnr_sb[:, 0:P], picked(t, n0, P), start=False, stop=False
+                    block[:, n0 : n0 + P], wnr_quarter[:, 0:P], picked(t, n0, P), start=False, stop=False
                 )
-        nc.tensor.matmul(block[:], wnr_sb[:, 0:P], picked(K - 1, 0, S), start=False, stop=True)
+        nc.tensor.matmul(block[:], wnr_quarter[:, 0:P], picked(K - 1, 0, S), start=False, stop=True)
         wide = held.tile([P, S], F32, name="wide")
-        nc.vector.tensor_scalar(wide[:], block[:], 1.0 / K, 0.0, MULT, MAX)
+        nc.vector.tensor_scalar_max(wide[:], block[:], 0.0)
         nc.sync.dma_start(out[0:P, :], wide[:])
 
         for h, total in enumerate(halves):
             for t in range(K):
                 nc.tensor.matmul(
-                    total[:], wnr_sb[:, P:M], picked(t, h * P, P), start=False, stop=t == K - 1
+                    total[:], wnr_quarter[:, P:M], picked(t, h * P, P), start=False, stop=t == K - 1
                 )
             result = held.tile([P, P], F32, name=f"result{h}")
-            nc.vector.tensor_scalar(result[:], total[:], 1.0 / K, 0.0, MULT, MAX)
+            nc.vector.tensor_scalar_max(result[:], total[:], 0.0)
             nc.sync.dma_start(out[P:M, h * P : (h + 1) * P], result[:])

@@ -22,12 +22,12 @@ def tile_residuesnetwork_kernel(tc, table, wr, wnr, offs, out):
         rows = [held.tile([P, P], BF16, name=f"rows{b}") for b in range(S // P)]
         for b in range(S // P):
             nc.sync.dma_start(rows[b][:], table[b * P : (b + 1) * P, :])
+        wr_sb = held.tile([P, M], BF16, name="wr_sb")
+        nc.sync.dma_start(wr_sb[:], wr)
         offsets = held.tile([P, N // PER_COLUMN], U16, name="offsets")
         nc.sync.dma_start(offsets[:], offs)
-        wr_sb = held.tile([P, M], BF16, name="wr_sb")
-        nc.scalar.dma_start(wr_sb[:], wr)
         wnr_sb = held.tile([P, M], BF16, name="wnr_sb")
-        nc.scalar.dma_start(wnr_sb[:], wnr)
+        nc.sync.dma_start(wnr_sb[:], wnr)
 
         wnr_quarter = held.tile([P, M], BF16, name="wnr_quarter")
         nc.scalar.mul(wnr_quarter[:], wnr_sb[:], 1.0 / K)

@@ -33,7 +33,8 @@ def tile_residuesnetwork_kernel(tc, table, wr, wnr, offs, out):
         nc.scalar.mul(wnr_quarter[:], wnr_sb[:], 1.0 / K)
 
         identity = held.tile([P, P], BF16, name="identity")
-        make_identity(nc, identity[:])
+        nc.vector.memset(identity[:], 0.0)
+        make_identity(nc, identity[:], nomemset=True)
         window = held.tile([P, S], BF16, name="window")
         for b in range(S // P):
             flipped = psum.tile([P, P], BF16, name=f"flipped{b}")

@@ -22,12 +22,12 @@ def tile_residuesnetwork_kernel(tc, table, wr, wnr, offs, out):
         rows = [held.tile([P, P], BF16, name=f"rows{b}") for b in range(S // P)]
         for b in range(S // P):
             nc.sync.dma_start(rows[b][:], table[b * P : (b + 1) * P, :])
+        wnr_sb = held.tile([P, M], BF16, name="wnr_sb")
+        nc.sync.dma_start(wnr_sb[:], wnr)
         wr_sb = held.tile([P, M], BF16, name="wr_sb")
         nc.sync.dma_start(wr_sb[:], wr)
         offsets = held.tile([P, N // PER_COLUMN], U16, name="offsets")
         nc.sync.dma_start(offsets[:], offs)
-        wnr_sb = held.tile([P, M], BF16, name="wnr_sb")
-        nc.sync.dma_start(wnr_sb[:], wnr)
 
         wnr_quarter = held.tile([P, M], BF16, name="wnr_quarter")
         nc.scalar.mul(wnr_quarter[:], wnr_sb[:], 1.0 / K)

import concourse.mybir as mybir
from concourse.masks import make_identity

BF16, F32, U16 = mybir.dt.bfloat16, mybir.dt.float32, mybir.dt.uint16

P = 128
S = 256
M = 256
K = 4
N = K * S
PER_COLUMN = 16

FLOPS = 2 * P * M * (S + N)


def tile_residuesnetwork_kernel(tc, table, wr, wnr, offs, out):
    nc = tc.nc
    with (
        tc.tile_pool(name="held", bufs=1) as held,
        tc.psum_pool(name="psum", bufs=1) as psum,
    ):
        rows = [held.tile([P, P], BF16, name=f"rows{b}") for b in range(S // P)]
        for b in range(S // P):
            nc.sync.dma_start(rows[b][:], table[b * P : (b + 1) * P, :])
        wnr_sb = held.tile([P, M], BF16, name="wnr_sb")
        nc.sync.dma_start(wnr_sb[:], wnr)
        wr_sb = held.tile([P, M], BF16, name="wr_sb")
        nc.sync.dma_start(wr_sb[:], wr)
        offsets = held.tile([P, N // PER_COLUMN], U16, name="offsets")
        nc.sync.dma_start(offsets[:], offs)

        wnr_quarter = held.tile([P, M], BF16, name="wnr_quarter")
        nc.scalar.mul(wnr_quarter[:], wnr_sb[:], 1.0 / K)

        identity = held.tile([P, P], BF16, name="identity")
        nc.vector.memset(identity[:], 0.0)
        make_identity(nc, identity[:], nomemset=True)
        window = held.tile([P, S], BF16, name="window")
        for b in range(S // P):
            flipped = psum.tile([P, P], BF16, name=f"flipped{b}")
            nc.tensor.transpose(flipped[:], rows[b][:], identity[:])
            nc.vector.tensor_copy(window[:, b * P : (b + 1) * P], flipped[:])

        def picked(t, n0, width):
            first = (t * S + n0) // PER_COLUMN
            return window[:].indirect(offsets[:, first : first + width // PER_COLUMN])

        block = psum.tile([P, S], F32, name="block")
        halves = [psum.tile([P, P], F32, name=f"half{h}") for h in range(S // P)]

        for h, n0 in enumerate(range(0, S, P)):
            nc.tensor.matmul(
                block[:, n0 : n0 + P], wr_sb[:, 0:P], window[:, n0 : n0 + P], start=h == 0, stop=False
            )
            nc.tensor.matmul(halves[h][:], wr_sb[:, P:M], window[:, n0 : n0 + P], start=True, stop=False)

        for t in range(K - 1):
            for n0 in range(0, S, P):
                nc.tensor.matmul(
                    block[:, n0 : n0 + P], wnr_quarter[:, 0:P], picked(t, n0, P), start=False, stop=False
                )
        nc.tensor.matmul(block[:], wnr_quarter[:, 0:P], picked(K - 1, 0, S), start=False, stop=True)
        wide = held.tile([P, S], F32, name="wide")
        nc.vector.tensor_scalar_max(wide[:], block[:], 0.0)
        nc.sync.dma_start(out[0:P, :], wide[:])

        for h, total in enumerate(halves):
            for t in range(K):
                nc.tensor.matmul(
                    total[:], wnr_quarter[:, P:M], picked(t, h * P, P), start=False, stop=t == K - 1
                )
            result = held.tile([P, P], F32, name=f"result{h}")
            nc.vector.tensor_scalar_max(result[:], total[:], 0.0)
            nc.sync.dma_start(out[P:M, h * P : (h + 1) * P], result[:])
